import numpy as np
import ml_dtypes


def mxq(x, axis, fmt="e4m3"):
    dtype, down = {"e4m3": (ml_dtypes.float8_e4m3fn, 7), "e5m2": (ml_dtypes.float8_e5m2, 14)}[fmt]
    v = np.moveaxis(np.asarray(x, np.float32).astype(ml_dtypes.bfloat16).astype(np.float64), axis, -1)
    blocks = v.reshape(v.shape[:-1] + (-1, 32))
    amax = np.abs(blocks).max(-1, keepdims=True)
    byte = np.maximum(np.where(amax > 0, np.frexp(amax)[1] - 1 + 127, 0) - down, 1)
    scale = np.exp2(byte - 127.0)
    codes = (blocks / scale).astype(np.float32).astype(dtype).astype(np.float64)
    return np.moveaxis((codes * scale).reshape(v.shape), -1, axis)


WIDE = False


def mx_kscale(k):
    if not WIDE:
        return np.ones(k)
    levels = np.array([30, -30])
    if k % 512:
        return np.exp2(np.random.permutation(np.resize(levels, k // 32))).repeat(32)
    a = np.empty((k // 512, 16))
    for p in range(k // 512):
        a[p, :8] = np.random.permutation(np.resize(levels, 8))
        for g in range(8):
            far = levels[np.abs(levels - a[p, g]) >= 10]
            a[p, g + 8] = far[np.random.randint(len(far))]
    return np.exp2(a.ravel()).repeat(32)


BF16 = ml_dtypes.bfloat16


def bf(x):
    return np.asarray(x, np.float32).astype(BF16)


def f64(x):
    return np.asarray(x).astype(np.float64)


B, S, H, A, NH = 4, 128, 1536, 1536, 12
HD = A // NH
LN_EPS = 1e-5


def setup_inputs():
    s = mx_kscale(A)
    return {"ctx_heads": bf(np.random.standard_normal((B, NH, S, HD)) * s.reshape(NH, 1, HD)),
            "Wo": bf(np.random.standard_normal((H, A)) / np.sqrt(A) / s),
            "bo": bf(np.random.standard_normal(H) * 0.3),
            "features": bf(np.random.standard_normal((B, S, H))),
            "ln_g": bf(1.0 + 0.1 * np.random.standard_normal(H)),
            "ln_b": bf(0.2 * np.random.standard_normal(H))}


def reference(ctx_heads, Wo, bo, features, ln_g, ln_b):
    ctx = f64(ctx_heads).transpose(0, 2, 1, 3).reshape(B, S, A)
    p = (mxq(ctx, 2, "e5m2") @ mxq(f64(Wo), 1, "e4m3").T) + f64(bo)
    y = p + f64(features)
    mu = y.mean(-1, keepdims=True)
    var = y.var(-1, keepdims=True)
    return (y - mu) / np.sqrt(var + LN_EPS) * f64(ln_g) + f64(ln_b)

@@ -1,0 +1,250 @@
+from contextlib import ExitStack
+
+import concourse.mybir as mybir
+from concourse.masks import make_identity
+
+B, S, H, A, NH = 4, 128, 1536, 1536, 12
+LN_EPS = 1e-5
+FLOPS = 2 * B * S * H * A
+
+F32 = mybir.dt.float32
+BF16 = mybir.dt.bfloat16
+U32 = mybir.dt.uint32
+U8 = mybir.dt.uint8
+E4M3X4 = mybir.dt.float8_e4m3fn_x4
+E5M2X4 = mybir.dt.float8_e5m2_x4
+ALU = mybir.AluOpType
+ACT = mybir.ActivationFunctionType
+AX = mybir.AxisListType
+
+P = 128
+K_PASS = 512
+N_TILE = 512
+PASSES = A // K_PASS
+CHUNKS = H // N_TILE
+
+
+def tile_hierarchicalattention_pb_kernel(tc, ctx_heads, Wo, bo, features, ln_g, ln_b, out):
+    nc = tc.nc
+    with ExitStack() as ctx:
+        const = ctx.enter_context(tc.tile_pool(name="const", bufs=1))
+        raw = ctx.enter_context(tc.tile_pool(name="raw", bufs=1))
+        stage = ctx.enter_context(tc.tile_pool(name="stage", bufs=6))
+        keep = ctx.enter_context(tc.tile_pool(name="keep", bufs=1))
+        work = ctx.enter_context(tc.tile_pool(name="work", bufs=2))
+        small = ctx.enter_context(tc.tile_pool(name="small", bufs=4))
+        tp_pool = ctx.enter_context(tc.psum_pool(name="tp", bufs=5))
+        acc_pool = ctx.enter_context(tc.psum_pool(name="accp", bufs=3))
+        ctx.enter_context(tc.manual_schedule())
+
+        ident = const.tile([P, P], F32, name="ident")
+        make_identity(nc, ident[:])
+        tiny = const.tile([P, 2], F32, name="tiny")
+        nc.vector.memset(tiny[:], 0.0)
+        nc.scalar.activation(out=tiny[:, 1:2], in_=tiny[:, 0:1], func=ACT.Square)
+        vrow = const.tile([P, H], BF16, name="vrow")
+        nc.vector.memset(vrow[:], 0.0)
+        sel = const.tile([P, 3, P], BF16, name="sel")
+        nc.vector.memset(sel[:], 0.0)
+        for j, vec in enumerate((bo, ln_g, ln_b)):
+            nc.scalar.dma_start(out=vrow[32 * j : 32 * j + 1, :], in_=vec.rearrange("(o n) -> o n", o=1))
+            nc.vector.memset(sel[32 * j : 32 * j + 1, j, :], 1.0)
+        mhalf = const.tile([P, 1], F32, name="mhalf")
+        nc.vector.memset(mhalf[:], -0.5)
+
+        x_raw = [raw.tile([P, A], BF16, name="x_raw%d" % b) for b in range(B)]
+        w_raw = [[raw.tile([P, A], BF16, name="w_raw%d_%d" % (c, a)) for a in range(4)] for c in range(CHUNKS)]
+        f_raw = [raw.tile([P, B, N_TILE], BF16, name="f_raw%d" % c) for c in range(CHUNKS)]
+
+        def load_x(b):
+            nc.sync.dma_start(
+                out=x_raw[b][:].rearrange("p (h d) -> p h d", h=NH),
+                in_=ctx_heads[b].rearrange("h s d -> s h d"),
+            )
+
+        def load_w(c):
+            for a in range(4):
+                r0 = N_TILE * c + P * a
+                nc.sync.dma_start(out=w_raw[c][a][:], in_=Wo[r0 : r0 + P, :])
+
+        def load_f(c):
+            nc.sync.dma_start(
+                out=f_raw[c][:],
+                in_=features.rearrange("b s n -> s b n")[:, :, N_TILE * c : N_TILE * (c + 1)],
+            )
+
+        load_w(0)
+        for b in range(B):
+            load_x(b)
+        load_f(0)
+        load_w(1)
+        load_f(1)
+        load_w(2)
+        load_f(2)
+
+        bc = const.tile([P, 3 * H], BF16, name="bc")
+
+        def broadcast_vectors():
+            for i in range(5):
+                q_list = [q for q in (2 * i, 2 * i + 1) if q < 9]
+                pb = tp_pool.tile([P, 1024], BF16, name="pb", tag="tp")
+                for q in q_list:
+                    j, c = divmod(q, 3)
+                    o0 = N_TILE * (q - 2 * i)
+                    nc.tensor.matmul(
+                        out=pb[:, o0 : o0 + N_TILE],
+                        lhsT=sel[:, j, :],
+                        rhs=vrow[:, N_TILE * c : N_TILE * (c + 1)],
+                        start=True,
+                        stop=True,
+                    )
+                ncol = N_TILE * len(q_list)
+                nc.scalar.copy(out=bc[:, 1024 * i : 1024 * i + ncol], in_=pb[:, :ncol])
+
+        fb = [keep.tile([P, H], F32, name="fb%d" % b) for b in range(B)]
+
+        def add_bias(c):
+            cs = slice(N_TILE * c, N_TILE * (c + 1))
+            for b in range(B):
+                nc.gpsimd.tensor_tensor(out=fb[b][:, cs], in0=f_raw[c][:, b, :], in1=bc[:, cs], op=ALU.add)
+
+        x_codes = [keep.tile([P, N_TILE], U32, name="x_codes%d" % g, align_bytes=64) for g in range(PASSES)]
+        x_scales = [keep.tile([P, N_TILE], U8, name="x_scales%d" % g, align_bytes=64) for g in range(PASSES)]
+        w_codes = [
+            [keep.tile([P, N_TILE], U32, name="w_codes%d_%d" % (c, g), align_bytes=64) for g in range(PASSES)]
+            for c in range(CHUNKS)
+        ]
+        w_scales = [
+            [keep.tile([P, N_TILE], U8, name="w_scales%d_%d" % (c, g), align_bytes=64) for g in range(PASSES)]
+            for c in range(CHUNKS)
+        ]
+        y = [keep.tile([P, H], F32, name="y%d" % b) for b in range(B)]
+        stats = [keep.tile([P, 2, CHUNKS], F32, name="stats%d" % b) for b in range(B)]
+        negc = [keep.tile([P, 1], F32, name="negc%d" % b) for b in range(B)]
+
+        def prepare(srcs, codes, scales, fmt, half, vector_passes):
+            banks = []
+            for g in range(PASSES):
+                tp = tp_pool.tile([P, 2, 2, P], F32, name="tp", tag="tp")
+                for a in range(2):
+                    words = srcs[a][:, K_PASS * g : K_PASS * (g + 1)].bitcast(F32)
+                    for u in range(2):
+                        nc.tensor.transpose(tp[:, a, u, :], words[:, u : K_PASS // 2 : 2], ident[:])
+                banks.append(tp)
+            groups = []
+            for g in range(PASSES):
+                grouped = stage.tile([P, 2 * N_TILE], BF16, name="grouped", align_bytes=64)
+                dst = grouped[:].bitcast(F32).rearrange("p (a r u) -> p a r u", a=2, u=2)
+                src = banks[g][:].rearrange("p a u r -> p a r u")
+                if g in vector_passes:
+                    nc.vector.tensor_copy(out=dst, in_=src)
+                else:
+                    nc.scalar.copy(out=dst, in_=src)
+                groups.append(grouped)
+            hs = slice(256 * half, 256 * (half + 1))
+            for g in range(PASSES):
+                nc.vector.quantize_mx(out=codes[g][:, hs].bitcast(fmt), scales=scales[g][:, hs], in_=groups[g][:])
+
+        def prepare_x(half, vector_passes):
+            prepare(x_raw[2 * half : 2 * half + 2], x_codes, x_scales, E5M2X4, half, vector_passes)
+
+        def prepare_w(c, half, vector_passes):
+            prepare(w_raw[c][2 * half : 2 * half + 2], w_codes[c], w_scales[c], E4M3X4, half, vector_passes)
+
+        acc = {}
+
+        def multiply(c, b):
+            acc[b] = acc_pool.tile([P, N_TILE], F32, name="acc", tag="acc")
+            ts = slice(P * b, P * (b + 1))
+            for g in range(PASSES):
+                nc.tensor.matmul_mx(
+                    out=acc[b][:],
+                    lhsT=x_codes[g][:, ts].bitcast(E5M2X4),
+                    lhsT_scale=x_scales[g][:, ts],
+                    rhs=w_codes[c][g][:].bitcast(E4M3X4),
+                    rhs_scale=w_scales[c][g][:],
+                    start=(g == 0),
+                    stop=(g == PASSES - 1),
+                )
+
+        def evacuate(c, b):
+            cs = slice(N_TILE * c, N_TILE * (c + 1))
+            nc.vector.scalar_tensor_tensor(
+                out=y[b][:, cs],
+                in0=acc[b][:],
+                scalar=1.0,
+                in1=fb[b][:, cs],
+                op0=ALU.mult,
+                op1=ALU.add,
+                accum_out=stats[b][:, 0, c : c + 1],
+            )
+            if c == 0:
+                nc.vector.tensor_scalar(
+                    out=negc[b][:], in0=stats[b][:, 0, 0:1], scalar1=-1.0 / N_TILE, scalar2=None, op0=ALU.mult
+                )
+            junk = work.tile([P, N_TILE], BF16, name="junk")
+            nc.scalar.activation(
+                out=junk[:],
+                in_=y[b][:, cs],
+                func=ACT.Square,
+                bias=negc[b][:],
+                scale=1.0,
+                accum_out=stats[b][:, 1, c : c + 1],
+            )
+
+        def finish(b):
+            red = small.tile([P, 2], F32, name="red")
+            nc.vector.tensor_reduce(out=red[:], in_=stats[b][:], axis=AX.X, op=ALU.add)
+            ms = small.tile([P, 2], F32, name="ms")
+            nc.vector.tensor_scalar(out=ms[:], in0=red[:], scalar1=1.0 / H, scalar2=None, op0=ALU.mult)
+            dev = small.tile([P, 1], F32, name="dev")
+            nc.vector.tensor_tensor(out=dev[:], in0=ms[:, 0:1], in1=negc[b][:], op=ALU.add)
+            dev2 = small.tile([P, 1], F32, name="dev2")
+            nc.vector.tensor_scalar(
+                out=dev2[:], in0=dev[:], scalar1=dev[:, 0:1], scalar2=LN_EPS, op0=ALU.mult, op1=ALU.subtract
+            )
+            ve = small.tile([P, 1], F32, name="ve")
+            nc.vector.tensor_tensor(out=ve[:], in0=ms[:, 1:2], in1=dev2[:], op=ALU.subtract)
+            rstd = small.tile([P, 1], F32, name="rstd")
+            nc.gpsimd.tensor_tensor(out=rstd[:], in0=ve[:], in1=mhalf[:], op=ALU.pow)
+            t = work.tile([P, H], F32, name="t")
+            nc.vector.scalar_tensor_tensor(
+                out=t[:], in0=y[b][:], scalar=ms[:, 0:1], in1=bc[:, H : 2 * H], op0=ALU.subtract, op1=ALU.mult
+            )
+            o = work.tile([P, H], F32, name="o")
+            for hs in (slice(0, H // 2), slice(H // 2, H)):
+                nc.vector.scalar_tensor_tensor(
+                    out=o[:, hs],
+                    in0=t[:, hs],
+                    scalar=rstd[:, 0:1],
+                    in1=bc[:, 2 * H + hs.start : 2 * H + hs.stop],
+                    op0=ALU.mult,
+                    op1=ALU.add,
+                )
+                nc.sync.dma_start(out=out[b, :, hs], in_=o[:, hs])
+
+        prepare_w(0, 0, (1,))
+        prepare_w(0, 1, (1,))
+        broadcast_vectors()
+        add_bias(0)
+        prepare_x(0, (1,))
+        prepare_x(1, (1,))
+        for c in (1, 2):
+            for half in range(2):
+                prepare_w(c, half, (1,))
+                for b in (2 * half, 2 * half + 1):
+                    multiply(c - 1, b)
+                for b in (2 * half, 2 * half + 1):
+                    evacuate(c - 1, b)
+                if half == 0:
+                    add_bias(c)
+        for b in range(B):
+            multiply(2, b)
+        evacuate(2, 0)
+        evacuate(2, 1)
+        finish(0)
+        evacuate(2, 2)
+        finish(1)
+        evacuate(2, 3)
+        finish(2)
+        finish(3)

@@ -22,6 +22,7 @@ K_PASS = 512
 N_TILE = 512
 PASSES = A // K_PASS
 CHUNKS = H // N_TILE
+SCALAR_COLS = N_TILE
 
 
 def tile_hierarchicalattention_pb_kernel(tc, ctx_heads, Wo, bo, features, ln_g, ln_b, out):
@@ -32,25 +33,26 @@ def tile_hierarchicalattention_pb_kernel(tc, ctx_heads, Wo, bo, features, ln_g, 
         stage = ctx.enter_context(tc.tile_pool(name="stage", bufs=6))
         keep = ctx.enter_context(tc.tile_pool(name="keep", bufs=1))
         work = ctx.enter_context(tc.tile_pool(name="work", bufs=2))
-        small = ctx.enter_context(tc.tile_pool(name="small", bufs=4))
+        small = ctx.enter_context(tc.tile_pool(name="small", bufs=2))
         tp_pool = ctx.enter_context(tc.psum_pool(name="tp", bufs=5))
         acc_pool = ctx.enter_context(tc.psum_pool(name="accp", bufs=3))
-        ctx.enter_context(tc.manual_schedule())
 
-        ident = const.tile([P, P], F32, name="ident")
-        make_identity(nc, ident[:])
-        tiny = const.tile([P, 2], F32, name="tiny")
-        nc.vector.memset(tiny[:], 0.0)
-        nc.scalar.activation(out=tiny[:, 1:2], in_=tiny[:, 0:1], func=ACT.Square)
         vrow = const.tile([P, H], BF16, name="vrow")
         nc.vector.memset(vrow[:], 0.0)
+        gb_rows = const.tile([P, P], BF16, name="gb_rows")
+        nc.vector.memset(gb_rows[:], 0.0)
+        ident = const.tile([P, P], F32, name="ident")
+        make_identity(nc, ident[:])
+        ident_bf = const.tile([P, P], BF16, name="ident_bf")
+        make_identity(nc, ident_bf[:])
+        tiny = const.tile([P, 2], F32, name="tiny")
+        nc.vector.memset(tiny[:], 1.0)
+        nc.scalar.activation(out=tiny[:, 1:2], in_=tiny[:, 0:1], func=ACT.Abs_reciprocal_sqrt)
         sel = const.tile([P, 3, P], BF16, name="sel")
         nc.vector.memset(sel[:], 0.0)
-        for j, vec in enumerate((bo, ln_g, ln_b)):
-            nc.scalar.dma_start(out=vrow[32 * j : 32 * j + 1, :], in_=vec.rearrange("(o n) -> o n", o=1))
+        for j in range(3):
             nc.vector.memset(sel[32 * j : 32 * j + 1, j, :], 1.0)
-        mhalf = const.tile([P, 1], F32, name="mhalf")
-        nc.vector.memset(mhalf[:], -0.5)
+        gb_col = const.tile([P, P], F32, name="gb_col")
 
         x_raw = [raw.tile([P, A], BF16, name="x_raw%d" % b) for b in range(B)]
         w_raw = [[raw.tile([P, A], BF16, name="w_raw%d_%d" % (c, a)) for a in range(4)] for c in range(CHUNKS)]
@@ -73,40 +75,51 @@ def tile_hierarchicalattention_pb_kernel(tc, ctx_heads, Wo, bo, features, ln_g, 
                 in_=features.rearrange("b s n -> s b n")[:, :, N_TILE * c : N_TILE * (c + 1)],
             )
 
-        load_w(0)
-        for b in range(B):
-            load_x(b)
-        load_f(0)
-        load_w(1)
-        load_f(1)
-        load_w(2)
-        load_f(2)
+        with tc.manual_schedule(engines={mybir.EngineType.SP}):
+            load_w(0)
+            for j, vec in enumerate((bo, ln_g, ln_b)):
+                nc.sync.dma_start(out=vrow[32 * j : 32 * j + 1, :], in_=vec.rearrange("(o n) -> o n", o=1))
+            nc.sync.dma_start(out=gb_rows[0:12, :], in_=ln_g.rearrange("(j p) -> j p", p=P))
+            nc.sync.dma_start(out=gb_rows[32:44, :], in_=ln_b.rearrange("(j p) -> j p", p=P))
+            load_f(0)
+            for b in range(B):
+                load_x(b)
+            load_w(1)
+            load_f(1)
+            load_w(2)
+            load_f(2)
 
-        bc = const.tile([P, 3 * H], BF16, name="bc")
+        ctx.enter_context(tc.manual_schedule(engines={mybir.EngineType.PE}))
+
+        BC_CHUNKS = [(0, 0), (0, 1), (0, 2), (1, 1), (1, 2), (2, 1), (2, 2)]
+        G0 = H
+        B0 = H + (H - SCALAR_COLS)
+        bc = const.tile([P, N_TILE * len(BC_CHUNKS)], BF16, name="bc")
 
         def broadcast_vectors():
-            for i in range(5):
-                q_list = [q for q in (2 * i, 2 * i + 1) if q < 9]
+            pcol = tp_pool.tile([P, P], BF16, name="pcol", tag="tp")
+            nc.tensor.transpose(pcol[:], gb_rows[:], ident_bf[:])
+            nc.vector.tensor_copy(out=gb_col[:], in_=pcol[:])
+            for i in range(0, len(BC_CHUNKS), 2):
+                pair = BC_CHUNKS[i : i + 2]
                 pb = tp_pool.tile([P, 1024], BF16, name="pb", tag="tp")
-                for q in q_list:
-                    j, c = divmod(q, 3)
-                    o0 = N_TILE * (q - 2 * i)
+                for k, (j, c) in enumerate(pair):
                     nc.tensor.matmul(
-                        out=pb[:, o0 : o0 + N_TILE],
+                        out=pb[:, N_TILE * k : N_TILE * (k + 1)],
                         lhsT=sel[:, j, :],
                         rhs=vrow[:, N_TILE * c : N_TILE * (c + 1)],
                         start=True,
                         stop=True,
                     )
-                ncol = N_TILE * len(q_list)
-                nc.scalar.copy(out=bc[:, 1024 * i : 1024 * i + ncol], in_=pb[:, :ncol])
+                ncol = N_TILE * len(pair)
+                nc.scalar.copy(out=bc[:, N_TILE * i : N_TILE * i + ncol], in_=pb[:, :ncol])
 
         fb = [keep.tile([P, H], F32, name="fb%d" % b) for b in range(B)]
 
-        def add_bias(c):
+        def add_bias(c, engine):
             cs = slice(N_TILE * c, N_TILE * (c + 1))
             for b in range(B):
-                nc.gpsimd.tensor_tensor(out=fb[b][:, cs], in0=f_raw[c][:, b, :], in1=bc[:, cs], op=ALU.add)
+                engine.tensor_tensor(out=fb[b][:, cs], in0=f_raw[c][:, b, :], in1=bc[:, cs], op=ALU.add)
 
         x_codes = [keep.tile([P, N_TILE], U32, name="x_codes%d" % g, align_bytes=64) for g in range(PASSES)]
         x_scales = [keep.tile([P, N_TILE], U8, name="x_scales%d" % g, align_bytes=64) for g in range(PASSES)]
@@ -119,8 +132,8 @@ def tile_hierarchicalattention_pb_kernel(tc, ctx_heads, Wo, bo, features, ln_g, 
             for c in range(CHUNKS)
         ]
         y = [keep.tile([P, H], F32, name="y%d" % b) for b in range(B)]
-        stats = [keep.tile([P, 2, CHUNKS], F32, name="stats%d" % b) for b in range(B)]
-        negc = [keep.tile([P, 1], F32, name="negc%d" % b) for b in range(B)]
+        stats = keep.tile([P, 2, B, CHUNKS], F32, name="stats")
+        negc = keep.tile([P, B], F32, name="negc")
 
         def prepare(srcs, codes, scales, fmt, half, vector_passes):
             banks = []
@@ -176,75 +189,164 @@ def tile_hierarchicalattention_pb_kernel(tc, ctx_heads, Wo, bo, features, ln_g, 
                 in1=fb[b][:, cs],
                 op0=ALU.mult,
                 op1=ALU.add,
-                accum_out=stats[b][:, 0, c : c + 1],
+                accum_out=stats[:, 0, b, c : c + 1],
             )
             if c == 0:
                 nc.vector.tensor_scalar(
-                    out=negc[b][:], in0=stats[b][:, 0, 0:1], scalar1=-1.0 / N_TILE, scalar2=None, op0=ALU.mult
+                    out=negc[:, b : b + 1], in0=stats[:, 0, b, 0:1], scalar1=-1.0 / N_TILE, scalar2=None, op0=ALU.mult
                 )
             junk = work.tile([P, N_TILE], BF16, name="junk")
             nc.scalar.activation(
                 out=junk[:],
                 in_=y[b][:, cs],
                 func=ACT.Square,
-                bias=negc[b][:],
+                bias=negc[:, b : b + 1],
                 scale=1.0,
-                accum_out=stats[b][:, 1, c : c + 1],
+                accum_out=stats[:, 1, b, c : c + 1],
             )
 
-        def finish(b):
-            red = small.tile([P, 2], F32, name="red")
-            nc.vector.tensor_reduce(out=red[:], in_=stats[b][:], axis=AX.X, op=ALU.add)
-            ms = small.tile([P, 2], F32, name="ms")
-            nc.vector.tensor_scalar(out=ms[:], in0=red[:], scalar1=1.0 / H, scalar2=None, op0=ALU.mult)
-            dev = small.tile([P, 1], F32, name="dev")
-            nc.vector.tensor_tensor(out=dev[:], in0=ms[:, 0:1], in1=negc[b][:], op=ALU.add)
-            dev2 = small.tile([P, 1], F32, name="dev2")
-            nc.vector.tensor_scalar(
-                out=dev2[:], in0=dev[:], scalar1=dev[:, 0:1], scalar2=LN_EPS, op0=ALU.mult, op1=ALU.subtract
-            )
-            ve = small.tile([P, 1], F32, name="ve")
-            nc.vector.tensor_tensor(out=ve[:], in0=ms[:, 1:2], in1=dev2[:], op=ALU.subtract)
-            rstd = small.tile([P, 1], F32, name="rstd")
-            nc.gpsimd.tensor_tensor(out=rstd[:], in0=ve[:], in1=mhalf[:], op=ALU.pow)
-            t = work.tile([P, H], F32, name="t")
+        moments = {}
+        z_tiles = {}
+        zt_banks = {}
+        ot_tiles = {}
+        back_banks = {}
+
+        part = keep.tile([P, 2, B], F32, name="part")
+        dev01 = keep.tile([P, B], F32, name="dev01")
+        var01 = keep.tile([P, B], F32, name="var01")
+
+        def partial_statistics():
+            red = small.tile([P, 2, B], F32, name="red")
+            nc.vector.tensor_reduce(out=red[:], in_=stats[:, :, :, 0:2], axis=AX.X, op=ALU.add)
+            nc.vector.tensor_scalar(out=part[:], in0=red[:], scalar1=1.0 / H, scalar2=None, op0=ALU.mult)
+            nc.vector.tensor_tensor(out=dev01[:], in0=part[:, 0, :], in1=negc[:], op=ALU.add)
+            nc.vector.tensor_scalar(out=var01[:], in0=part[:, 1, :], scalar1=LN_EPS, scalar2=None, op0=ALU.add)
+
+        def statistics(b0):
+            bs = slice(b0, b0 + 2)
+            mean = small.tile([P, 2], F32, name="mean")
             nc.vector.scalar_tensor_tensor(
-                out=t[:], in0=y[b][:], scalar=ms[:, 0:1], in1=bc[:, H : 2 * H], op0=ALU.subtract, op1=ALU.mult
+                out=mean[:], in0=stats[:, 0, bs, 2], scalar=1.0 / H, in1=part[:, 0, bs], op0=ALU.mult, op1=ALU.add
             )
-            o = work.tile([P, H], F32, name="o")
-            for hs in (slice(0, H // 2), slice(H // 2, H)):
-                nc.vector.scalar_tensor_tensor(
-                    out=o[:, hs],
-                    in0=t[:, hs],
-                    scalar=rstd[:, 0:1],
-                    in1=bc[:, 2 * H + hs.start : 2 * H + hs.stop],
-                    op0=ALU.mult,
-                    op1=ALU.add,
+            dev = small.tile([P, 2], F32, name="dev")
+            nc.vector.scalar_tensor_tensor(
+                out=dev[:], in0=stats[:, 0, bs, 2], scalar=1.0 / H, in1=dev01[:, bs], op0=ALU.mult, op1=ALU.add
+            )
+            dev2 = small.tile([P, 2], F32, name="dev2")
+            nc.vector.tensor_tensor(out=dev2[:], in0=dev[:], in1=dev[:], op=ALU.mult)
+            nvar = small.tile([P, 2], F32, name="nvar")
+            nc.vector.tensor_tensor(out=nvar[:], in0=dev2[:], in1=var01[:, bs], op=ALU.subtract)
+            rstd = small.tile([P, 2], F32, name="rstd")
+            for k in range(2):
+                nc.scalar.activation(
+                    out=rstd[:, k : k + 1],
+                    in_=stats[:, 1, b0 + k, 2:3],
+                    func=ACT.Abs_reciprocal_sqrt,
+                    bias=nvar[:, k : k + 1],
+                    scale=-1.0 / H,
                 )
-                nc.sync.dma_start(out=out[b, :, hs], in_=o[:, hs])
+            shift = small.tile([P, 2], F32, name="shift")
+            nc.vector.scalar_tensor_tensor(
+                out=shift[:], in0=mean[:], scalar=-1.0, in1=rstd[:], op0=ALU.mult, op1=ALU.mult
+            )
+            for k in range(2):
+                moments[b0 + k] = (mean[:, k : k + 1], rstd[:, k : k + 1], shift[:, k : k + 1])
 
-        prepare_w(0, 0, (1,))
-        prepare_w(0, 1, (1,))
+        def vector_share(b):
+            mean, rstd, shift = moments[b]
+            v0 = SCALAR_COLS
+            t = work.tile([P, H - SCALAR_COLS], F32, name="t")
+            nc.vector.scalar_tensor_tensor(
+                out=t[:], in0=y[b][:, v0:], scalar=mean, in1=bc[:, G0:B0], op0=ALU.subtract, op1=ALU.mult
+            )
+            o = work.tile([P, H - SCALAR_COLS], F32, name="o")
+            nc.vector.scalar_tensor_tensor(
+                out=o[:], in0=t[:], scalar=rstd, in1=bc[:, B0:], op0=ALU.mult, op1=ALU.add
+            )
+            nc.sync.dma_start(out=out[b, :, v0:], in_=o[:])
+
+        def normalise(b):
+            mean, rstd, shift = moments[b]
+            z = work.tile([P, SCALAR_COLS], F32, name="z")
+            nc.scalar.activation(out=z[:], in_=y[b][:, :SCALAR_COLS], func=ACT.Identity, bias=shift, scale=rstd)
+            z_tiles[b] = z
+
+        def turn(b):
+            zt = tp_pool.tile([P, 4, P], F32, name="zt", tag="tp")
+            for j in range(4):
+                nc.tensor.transpose(zt[:, j, :], z_tiles[b][:, P * j : P * (j + 1)], ident[:])
+            zt_banks[b] = zt
+
+        def gain_and_bias(b):
+            ot = work.tile([P, 4, P], F32, name="ot")
+            for j in range(4):
+                nc.scalar.activation(
+                    out=ot[:, j, :],
+                    in_=zt_banks[b][:, j, :],
+                    func=ACT.Identity,
+                    bias=gb_col[:, 32 + j : 33 + j],
+                    scale=gb_col[:, j : j + 1],
+                )
+            ot_tiles[b] = ot
+
+        def turn_back(b):
+            bk = tp_pool.tile([P, 4, P], F32, name="bk", tag="tp")
+            for j in range(4):
+                nc.tensor.transpose(bk[:, j, :], ot_tiles[b][:, j, :], ident[:])
+            back_banks[b] = bk
+
+        def scalar_store(b):
+            o_s = work.tile([P, SCALAR_COLS], F32, name="o_s")
+            nc.scalar.copy(out=o_s[:], in_=back_banks[b][:].rearrange("p j r -> p (j r)"))
+            nc.sync.dma_start(out=out[b, :, :SCALAR_COLS], in_=o_s[:])
+
+        prepare_w(0, 0, (1, 2))
+        prepare_w(0, 1, (1, 2))
         broadcast_vectors()
-        add_bias(0)
+        add_bias(0, nc.vector)
         prepare_x(0, (1,))
         prepare_x(1, (1,))
-        for c in (1, 2):
-            for half in range(2):
-                prepare_w(c, half, (1,))
-                for b in (2 * half, 2 * half + 1):
-                    multiply(c - 1, b)
-                for b in (2 * half, 2 * half + 1):
-                    evacuate(c - 1, b)
-                if half == 0:
-                    add_bias(c)
+        add_bias(1, nc.gpsimd)
+        add_bias(2, nc.gpsimd)
+
+        def multiply_pair(c, half):
+            for b in (2 * half, 2 * half + 1):
+                multiply(c, b)
+            for b in (2 * half, 2 * half + 1):
+                evacuate(c, b)
+
+        multiply_pair(0, 0)
+        prepare_w(1, 0, (1,))
+        multiply_pair(0, 1)
+        prepare_w(1, 1, (1,))
+        prepare_w(2, 0, (1,))
+        multiply_pair(1, 0)
+        prepare_w(2, 1, (1,))
+        multiply_pair(1, 1)
+        partial_statistics()
         for b in range(B):
             multiply(2, b)
         evacuate(2, 0)
         evacuate(2, 1)
-        finish(0)
+        statistics(0)
         evacuate(2, 2)
-        finish(1)
         evacuate(2, 3)
-        finish(2)
-        finish(3)
+        for b in (0, 1):
+            normalise(b)
+            turn(b)
+        statistics(2)
+        for b in (0, 1):
+            gain_and_bias(b)
+            turn_back(b)
+        for b in (2, 3):
+            normalise(b)
+            turn(b)
+        for b in (0, 1):
+            scalar_store(b)
+            vector_share(b)
+        for b in (2, 3):
+            gain_and_bias(b)
+            turn_back(b)
+        for b in (2, 3):
+            vector_share(b)
+            scalar_store(b)

@@ -48,11 +48,12 @@ def tile_hierarchicalattention_pb_kernel(tc, ctx_heads, Wo, bo, features, ln_g, 
         tiny = const.tile([P, 2], F32, name="tiny")
         nc.vector.memset(tiny[:], 1.0)
         nc.scalar.activation(out=tiny[:, 1:2], in_=tiny[:, 0:1], func=ACT.Abs_reciprocal_sqrt)
-        sel = const.tile([P, 3, P], BF16, name="sel")
+        sel = const.tile([P, 1, P], BF16, name="sel")
         nc.vector.memset(sel[:], 0.0)
-        for j in range(3):
-            nc.vector.memset(sel[32 * j : 32 * j + 1, j, :], 1.0)
+        nc.vector.memset(sel[0:1, 0, :], 1.0)
         gb_col = const.tile([P, P], F32, name="gb_col")
+        g_bc = const.tile([P, H - SCALAR_COLS], BF16, name="g_bc")
+        b_bc = const.tile([P, H - SCALAR_COLS], BF16, name="b_bc")
 
         x_raw = [raw.tile([P, A], BF16, name="x_raw%d" % b) for b in range(B)]
         w_raw = [[raw.tile([P, A], BF16, name="w_raw%d_%d" % (c, a)) for a in range(4)] for c in range(CHUNKS)]
@@ -64,8 +65,8 @@ def tile_hierarchicalattention_pb_kernel(tc, ctx_heads, Wo, bo, features, ln_g, 
                 in_=ctx_heads[b].rearrange("h s d -> s h d"),
             )
 
-        def load_w(c):
-            for a in range(4):
+        def load_w(c, half):
+            for a in (2 * half, 2 * half + 1):
                 r0 = N_TILE * c + P * a
                 nc.sync.dma_start(out=w_raw[c][a][:], in_=Wo[r0 : r0 + P, :])
 
@@ -76,24 +77,28 @@ def tile_hierarchicalattention_pb_kernel(tc, ctx_heads, Wo, bo, features, ln_g, 
             )
 
         with tc.manual_schedule(engines={mybir.EngineType.SP}):
-            load_w(0)
-            for j, vec in enumerate((bo, ln_g, ln_b)):
-                nc.sync.dma_start(out=vrow[32 * j : 32 * j + 1, :], in_=vec.rearrange("(o n) -> o n", o=1))
+            load_w(0, 0)
+            load_w(0, 1)
+            nc.sync.dma_start(out=vrow[0:1, :], in_=bo.rearrange("(o n) -> o n", o=1))
             nc.sync.dma_start(out=gb_rows[0:12, :], in_=ln_g.rearrange("(j p) -> j p", p=P))
             nc.sync.dma_start(out=gb_rows[32:44, :], in_=ln_b.rearrange("(j p) -> j p", p=P))
+            load_x(0)
+            load_x(1)
             load_f(0)
-            for b in range(B):
-                load_x(b)
-            load_w(1)
+            load_w(1, 0)
+            load_x(2)
+            load_x(3)
+            load_w(1, 1)
             load_f(1)
-            load_w(2)
+            load_w(2, 0)
+            load_w(2, 1)
             load_f(2)
+            nc.sync.dma_start(out=g_bc[:], in_=ln_g[SCALAR_COLS:].partition_broadcast(P))
+            nc.sync.dma_start(out=b_bc[:], in_=ln_b[SCALAR_COLS:].partition_broadcast(P))
 
         ctx.enter_context(tc.manual_schedule(engines={mybir.EngineType.PE}))
 
-        BC_CHUNKS = [(0, 0), (0, 1), (0, 2), (1, 1), (1, 2), (2, 1), (2, 2)]
-        G0 = H
-        B0 = H + (H - SCALAR_COLS)
+        BC_CHUNKS = [(0, 0), (0, 1), (0, 2)]
         bc = const.tile([P, N_TILE * len(BC_CHUNKS)], BF16, name="bc")
 
         def broadcast_vectors():
@@ -136,14 +141,12 @@ def tile_hierarchicalattention_pb_kernel(tc, ctx_heads, Wo, bo, features, ln_g, 
         negc = keep.tile([P, B], F32, name="negc")
 
         def prepare(srcs, codes, scales, fmt, half, vector_passes):
-            banks = []
-            for g in range(PASSES):
-                tp = tp_pool.tile([P, 2, 2, P], F32, name="tp", tag="tp")
-                for a in range(2):
+            banks = [tp_pool.tile([P, 2, 2, P], F32, name="tp%d" % g, tag="tp") for g in range(PASSES)]
+            for a in range(2):
+                for g in range(PASSES):
                     words = srcs[a][:, K_PASS * g : K_PASS * (g + 1)].bitcast(F32)
                     for u in range(2):
-                        nc.tensor.transpose(tp[:, a, u, :], words[:, u : K_PASS // 2 : 2], ident[:])
-                banks.append(tp)
+                        nc.tensor.transpose(banks[g][:, a, u, :], words[:, u : K_PASS // 2 : 2], ident[:])
             groups = []
             for g in range(PASSES):
                 grouped = stage.tile([P, 2 * N_TILE], BF16, name="grouped", align_bytes=64)
@@ -257,11 +260,11 @@ def tile_hierarchicalattention_pb_kernel(tc, ctx_heads, Wo, bo, features, ln_g, 
             v0 = SCALAR_COLS
             t = work.tile([P, H - SCALAR_COLS], F32, name="t")
             nc.vector.scalar_tensor_tensor(
-                out=t[:], in0=y[b][:, v0:], scalar=mean, in1=bc[:, G0:B0], op0=ALU.subtract, op1=ALU.mult
+                out=t[:], in0=y[b][:, v0:], scalar=mean, in1=g_bc[:], op0=ALU.subtract, op1=ALU.mult
             )
             o = work.tile([P, H - SCALAR_COLS], F32, name="o")
             nc.vector.scalar_tensor_tensor(
-                out=o[:], in0=t[:], scalar=rstd, in1=bc[:, B0:], op0=ALU.mult, op1=ALU.add
+                out=o[:], in0=t[:], scalar=rstd, in1=b_bc[:], op0=ALU.mult, op1=ALU.add
             )
             nc.sync.dma_start(out=out[b, :, v0:], in_=o[:])
 
@@ -304,8 +307,6 @@ def tile_hierarchicalattention_pb_kernel(tc, ctx_heads, Wo, bo, features, ln_g, 
         prepare_w(0, 1, (1, 2))
         broadcast_vectors()
         add_bias(0, nc.vector)
-        prepare_x(0, (1,))
-        prepare_x(1, (1,))
         add_bias(1, nc.gpsimd)
         add_bias(2, nc.gpsimd)
 
@@ -315,13 +316,15 @@ def tile_hierarchicalattention_pb_kernel(tc, ctx_heads, Wo, bo, features, ln_g, 
             for b in (2 * half, 2 * half + 1):
                 evacuate(c, b)
 
-        multiply_pair(0, 0)
+        prepare_x(0, (1,))
         prepare_w(1, 0, (1,))
-        multiply_pair(0, 1)
+        multiply_pair(0, 0)
+        prepare_x(1, (1,))
         prepare_w(1, 1, (1,))
+        multiply_pair(0, 1)
         prepare_w(2, 0, (1,))
-        multiply_pair(1, 0)
         prepare_w(2, 1, (1,))
+        multiply_pair(1, 0)
         multiply_pair(1, 1)
         partial_statistics()
         for b in range(B):

@@ -303,12 +303,10 @@ def tile_hierarchicalattention_pb_kernel(tc, ctx_heads, Wo, bo, features, ln_g, 
             nc.scalar.copy(out=o_s[:], in_=back_banks[b][:].rearrange("p j r -> p (j r)"))
             nc.sync.dma_start(out=out[b, :, :SCALAR_COLS], in_=o_s[:])
 
-        prepare_w(0, 0, (1, 2))
-        prepare_w(0, 1, (1, 2))
+        prepare_w(0, 0, (1,))
+        prepare_w(0, 1, (1,))
         broadcast_vectors()
         add_bias(0, nc.vector)
-        add_bias(1, nc.gpsimd)
-        add_bias(2, nc.gpsimd)
 
         def multiply_pair(c, half):
             for b in (2 * half, 2 * half + 1):
@@ -317,14 +315,16 @@ def tile_hierarchicalattention_pb_kernel(tc, ctx_heads, Wo, bo, features, ln_g, 
                 evacuate(c, b)
 
         prepare_x(0, (1,))
-        prepare_w(1, 0, (1,))
+        prepare_w(1, 0, ())
         multiply_pair(0, 0)
-        prepare_x(1, (1,))
-        prepare_w(1, 1, (1,))
+        prepare_x(1, ())
+        prepare_w(1, 1, ())
         multiply_pair(0, 1)
-        prepare_w(2, 0, (1,))
-        prepare_w(2, 1, (1,))
+        add_bias(1, nc.vector)
+        prepare_w(2, 0, ())
+        prepare_w(2, 1, ())
         multiply_pair(1, 0)
+        add_bias(2, nc.vector)
         multiply_pair(1, 1)
         partial_statistics()
         for b in range(B):

@@ -48,12 +48,11 @@ def tile_hierarchicalattention_pb_kernel(tc, ctx_heads, Wo, bo, features, ln_g, 
         tiny = const.tile([P, 2], F32, name="tiny")
         nc.vector.memset(tiny[:], 1.0)
         nc.scalar.activation(out=tiny[:, 1:2], in_=tiny[:, 0:1], func=ACT.Abs_reciprocal_sqrt)
-        sel = const.tile([P, 1, P], BF16, name="sel")
+        sel = const.tile([P, 3, P], BF16, name="sel")
         nc.vector.memset(sel[:], 0.0)
-        nc.vector.memset(sel[0:1, 0, :], 1.0)
+        for j in range(3):
+            nc.vector.memset(sel[32 * j : 32 * j + 1, j, :], 1.0)
         gb_col = const.tile([P, P], F32, name="gb_col")
-        g_bc = const.tile([P, H - SCALAR_COLS], BF16, name="g_bc")
-        b_bc = const.tile([P, H - SCALAR_COLS], BF16, name="b_bc")
 
         x_raw = [raw.tile([P, A], BF16, name="x_raw%d" % b) for b in range(B)]
         w_raw = [[raw.tile([P, A], BF16, name="w_raw%d_%d" % (c, a)) for a in range(4)] for c in range(CHUNKS)]
@@ -79,7 +78,8 @@ def tile_hierarchicalattention_pb_kernel(tc, ctx_heads, Wo, bo, features, ln_g, 
         with tc.manual_schedule(engines={mybir.EngineType.SP}):
             load_w(0, 0)
             load_w(0, 1)
-            nc.sync.dma_start(out=vrow[0:1, :], in_=bo.rearrange("(o n) -> o n", o=1))
+            for j, vec in enumerate((bo, ln_g, ln_b)):
+                nc.sync.dma_start(out=vrow[32 * j : 32 * j + 1, :], in_=vec.rearrange("(o n) -> o n", o=1))
             nc.sync.dma_start(out=gb_rows[0:12, :], in_=ln_g.rearrange("(j p) -> j p", p=P))
             nc.sync.dma_start(out=gb_rows[32:44, :], in_=ln_b.rearrange("(j p) -> j p", p=P))
             load_x(0)
@@ -93,8 +93,6 @@ def tile_hierarchicalattention_pb_kernel(tc, ctx_heads, Wo, bo, features, ln_g, 
             load_w(2, 0)
             load_w(2, 1)
             load_f(2)
-            nc.sync.dma_start(out=g_bc[:], in_=ln_g[SCALAR_COLS:].partition_broadcast(P))
-            nc.sync.dma_start(out=b_bc[:], in_=ln_b[SCALAR_COLS:].partition_broadcast(P))
 
         ctx.enter_context(tc.manual_schedule(engines={mybir.EngineType.PE}))
 
@@ -118,6 +116,21 @@ def tile_hierarchicalattention_pb_kernel(tc, ctx_heads, Wo, bo, features, ln_g, 
                     )
                 ncol = N_TILE * len(pair)
                 nc.scalar.copy(out=bc[:, N_TILE * i : N_TILE * i + ncol], in_=pb[:, :ncol])
+
+        gain_bias = {}
+
+        def broadcast_gain_and_bias():
+            for j in (1, 2):
+                pg = tp_pool.tile([P, H - SCALAR_COLS], BF16, name="pg%d" % j, tag="tp")
+                for k in range(2):
+                    nc.tensor.matmul(
+                        out=pg[:, N_TILE * k : N_TILE * (k + 1)],
+                        lhsT=sel[:, j, :],
+                        rhs=vrow[:, SCALAR_COLS + N_TILE * k : SCALAR_COLS + N_TILE * (k + 1)],
+                        start=True,
+                        stop=True,
+                    )
+                gain_bias[j] = pg
 
         fb = [keep.tile([P, H], F32, name="fb%d" % b) for b in range(B)]
 
@@ -260,11 +273,11 @@ def tile_hierarchicalattention_pb_kernel(tc, ctx_heads, Wo, bo, features, ln_g, 
             v0 = SCALAR_COLS
             t = work.tile([P, H - SCALAR_COLS], F32, name="t")
             nc.vector.scalar_tensor_tensor(
-                out=t[:], in0=y[b][:, v0:], scalar=mean, in1=g_bc[:], op0=ALU.subtract, op1=ALU.mult
+                out=t[:], in0=y[b][:, v0:], scalar=mean, in1=gain_bias[1][:], op0=ALU.subtract, op1=ALU.mult
             )
             o = work.tile([P, H - SCALAR_COLS], F32, name="o")
             nc.vector.scalar_tensor_tensor(
-                out=o[:], in0=t[:], scalar=rstd, in1=b_bc[:], op0=ALU.mult, op1=ALU.add
+                out=o[:], in0=t[:], scalar=rstd, in1=gain_bias[2][:], op0=ALU.mult, op1=ALU.add
             )
             nc.sync.dma_start(out=out[b, :, v0:], in_=o[:])
 
@@ -303,10 +316,12 @@ def tile_hierarchicalattention_pb_kernel(tc, ctx_heads, Wo, bo, features, ln_g, 
             nc.scalar.copy(out=o_s[:], in_=back_banks[b][:].rearrange("p j r -> p (j r)"))
             nc.sync.dma_start(out=out[b, :, :SCALAR_COLS], in_=o_s[:])
 
-        prepare_w(0, 0, (1,))
-        prepare_w(0, 1, (1,))
+        prepare_w(0, 0, (1, 2))
+        prepare_w(0, 1, (1, 2))
         broadcast_vectors()
         add_bias(0, nc.vector)
+        add_bias(1, nc.gpsimd)
+        add_bias(2, nc.gpsimd)
 
         def multiply_pair(c, half):
             for b in (2 * half, 2 * half + 1):
@@ -315,20 +330,19 @@ def tile_hierarchicalattention_pb_kernel(tc, ctx_heads, Wo, bo, features, ln_g, 
                 evacuate(c, b)
 
         prepare_x(0, (1,))
-        prepare_w(1, 0, ())
+        prepare_w(1, 0, (1,))
         multiply_pair(0, 0)
-        prepare_x(1, ())
-        prepare_w(1, 1, ())
+        prepare_x(1, (1,))
+        prepare_w(1, 1, (1,))
         multiply_pair(0, 1)
-        add_bias(1, nc.vector)
-        prepare_w(2, 0, ())
-        prepare_w(2, 1, ())
+        prepare_w(2, 0, (1,))
         multiply_pair(1, 0)
-        add_bias(2, nc.vector)
+        prepare_w(2, 1, (1,))
         multiply_pair(1, 1)
         partial_statistics()
         for b in range(B):
             multiply(2, b)
+        broadcast_gain_and_bias()
         evacuate(2, 0)
         evacuate(2, 1)
         statistics(0)

@@ -96,26 +96,25 @@ def tile_hierarchicalattention_pb_kernel(tc, ctx_heads, Wo, bo, features, ln_g, 
 
         ctx.enter_context(tc.manual_schedule(engines={mybir.EngineType.PE}))
 
-        BC_CHUNKS = [(0, 0), (0, 1), (0, 2)]
-        bc = const.tile([P, N_TILE * len(BC_CHUNKS)], BF16, name="bc")
+        bc = const.tile([P, H], BF16, name="bc")
 
-        def broadcast_vectors():
+        def columns_of_gain_and_bias():
             pcol = tp_pool.tile([P, P], BF16, name="pcol", tag="tp")
             nc.tensor.transpose(pcol[:], gb_rows[:], ident_bf[:])
             nc.vector.tensor_copy(out=gb_col[:], in_=pcol[:])
-            for i in range(0, len(BC_CHUNKS), 2):
-                pair = BC_CHUNKS[i : i + 2]
-                pb = tp_pool.tile([P, 1024], BF16, name="pb", tag="tp")
-                for k, (j, c) in enumerate(pair):
-                    nc.tensor.matmul(
-                        out=pb[:, N_TILE * k : N_TILE * (k + 1)],
-                        lhsT=sel[:, j, :],
-                        rhs=vrow[:, N_TILE * c : N_TILE * (c + 1)],
-                        start=True,
-                        stop=True,
-                    )
-                ncol = N_TILE * len(pair)
-                nc.scalar.copy(out=bc[:, N_TILE * i : N_TILE * i + ncol], in_=pb[:, :ncol])
+
+        def broadcast_bias(chunks):
+            pb = tp_pool.tile([P, 1024], BF16, name="pb", tag="tp")
+            for k, c in enumerate(chunks):
+                nc.tensor.matmul(
+                    out=pb[:, N_TILE * k : N_TILE * (k + 1)],
+                    lhsT=sel[:, 0, :],
+                    rhs=vrow[:, N_TILE * c : N_TILE * (c + 1)],
+                    start=True,
+                    stop=True,
+                )
+            ncol = N_TILE * len(chunks)
+            nc.scalar.copy(out=bc[:, N_TILE * chunks[0] : N_TILE * chunks[0] + ncol], in_=pb[:, :ncol])
 
         gain_bias = {}
 
@@ -153,13 +152,16 @@ def tile_hierarchicalattention_pb_kernel(tc, ctx_heads, Wo, bo, features, ln_g, 
         stats = keep.tile([P, 2, B, CHUNKS], F32, name="stats")
         negc = keep.tile([P, B], F32, name="negc")
 
-        def prepare(srcs, codes, scales, fmt, half, vector_passes):
-            banks = [tp_pool.tile([P, 2, 2, P], F32, name="tp%d" % g, tag="tp") for g in range(PASSES)]
-            for a in range(2):
-                for g in range(PASSES):
-                    words = srcs[a][:, K_PASS * g : K_PASS * (g + 1)].bitcast(F32)
-                    for u in range(2):
-                        nc.tensor.transpose(banks[g][:, a, u, :], words[:, u : K_PASS // 2 : 2], ident[:])
+        def begin():
+            return [tp_pool.tile([P, 2, 2, P], F32, name="tp%d" % g, tag="tp") for g in range(PASSES)]
+
+        def turn_rows(srcs, banks, a):
+            for g in range(PASSES):
+                words = srcs[a][:, K_PASS * g : K_PASS * (g + 1)].bitcast(F32)
+                for u in range(2):
+                    nc.tensor.transpose(banks[g][:, a, u, :], words[:, u : K_PASS // 2 : 2], ident[:])
+
+        def finish(banks, codes, scales, fmt, half, vector_passes):
             groups = []
             for g in range(PASSES):
                 grouped = stage.tile([P, 2 * N_TILE], BF16, name="grouped", align_bytes=64)
@@ -174,11 +176,29 @@ def tile_hierarchicalattention_pb_kernel(tc, ctx_heads, Wo, bo, features, ln_g, 
             for g in range(PASSES):
                 nc.vector.quantize_mx(out=codes[g][:, hs].bitcast(fmt), scales=scales[g][:, hs], in_=groups[g][:])
 
+        def x_rows(half):
+            return x_raw[2 * half : 2 * half + 2]
+
+        def w_rows(c, half):
+            return w_raw[c][2 * half : 2 * half + 2]
+
+        def finish_x(banks, half, vector_passes):
+            finish(banks, x_codes, x_scales, E5M2X4, half, vector_passes)
+
+        def finish_w(banks, c, half, vector_passes):
+            finish(banks, w_codes[c], w_scales[c], E4M3X4, half, vector_passes)
+
         def prepare_x(half, vector_passes):
-            prepare(x_raw[2 * half : 2 * half + 2], x_codes, x_scales, E5M2X4, half, vector_passes)
+            banks = begin()
+            turn_rows(x_rows(half), banks, 0)
+            turn_rows(x_rows(half), banks, 1)
+            finish_x(banks, half, vector_passes)
 
         def prepare_w(c, half, vector_passes):
-            prepare(w_raw[c][2 * half : 2 * half + 2], w_codes[c], w_scales[c], E4M3X4, half, vector_passes)
+            banks = begin()
+            turn_rows(w_rows(c, half), banks, 0)
+            turn_rows(w_rows(c, half), banks, 1)
+            finish_w(banks, c, half, vector_passes)
 
         acc = {}
 
@@ -316,29 +336,38 @@ def tile_hierarchicalattention_pb_kernel(tc, ctx_heads, Wo, bo, features, ln_g, 
             nc.scalar.copy(out=o_s[:], in_=back_banks[b][:].rearrange("p j r -> p (j r)"))
             nc.sync.dma_start(out=out[b, :, :SCALAR_COLS], in_=o_s[:])
 
+        def multiply_and_evacuate(c, b):
+            multiply(c, b)
+            evacuate(c, b)
+
         prepare_w(0, 0, (1, 2))
         prepare_w(0, 1, (1, 2))
-        broadcast_vectors()
+        columns_of_gain_and_bias()
+        broadcast_bias([0])
         add_bias(0, nc.vector)
+        prepare_x(0, (1,))
+        broadcast_bias([1, 2])
         add_bias(1, nc.gpsimd)
         add_bias(2, nc.gpsimd)
-
-        def multiply_pair(c, half):
-            for b in (2 * half, 2 * half + 1):
-                multiply(c, b)
-            for b in (2 * half, 2 * half + 1):
-                evacuate(c, b)
-
-        prepare_x(0, (1,))
         prepare_w(1, 0, (1,))
-        multiply_pair(0, 0)
+        multiply_and_evacuate(0, 0)
         prepare_x(1, (1,))
+        multiply_and_evacuate(0, 1)
         prepare_w(1, 1, (1,))
-        multiply_pair(0, 1)
-        prepare_w(2, 0, (1,))
-        multiply_pair(1, 0)
-        prepare_w(2, 1, (1,))
-        multiply_pair(1, 1)
+        multiply_and_evacuate(0, 2)
+        banks = begin()
+        turn_rows(w_rows(2, 0), banks, 0)
+        multiply_and_evacuate(0, 3)
+        turn_rows(w_rows(2, 0), banks, 1)
+        finish_w(banks, 2, 0, (1,))
+        multiply_and_evacuate(1, 0)
+        banks = begin()
+        turn_rows(w_rows(2, 1), banks, 0)
+        multiply_and_evacuate(1, 1)
+        turn_rows(w_rows(2, 1), banks, 1)
+        finish_w(banks, 2, 1, (1,))
+        multiply_and_evacuate(1, 2)
+        multiply_and_evacuate(1, 3)
         partial_statistics()
         for b in range(B):
             multiply(2, b)

@@ -349,17 +349,17 @@ def tile_hierarchicalattention_pb_kernel(tc, ctx_heads, Wo, bo, features, ln_g, 
         broadcast_bias([1, 2])
         add_bias(1, nc.gpsimd)
         add_bias(2, nc.gpsimd)
-        prepare_w(1, 0, (1,))
+        prepare_w(1, 0, ())
         multiply_and_evacuate(0, 0)
-        prepare_x(1, (1,))
+        prepare_x(1, ())
         multiply_and_evacuate(0, 1)
-        prepare_w(1, 1, (1,))
+        prepare_w(1, 1, ())
         multiply_and_evacuate(0, 2)
         banks = begin()
         turn_rows(w_rows(2, 0), banks, 0)
         multiply_and_evacuate(0, 3)
         turn_rows(w_rows(2, 0), banks, 1)
-        finish_w(banks, 2, 0, (1,))
+        finish_w(banks, 2, 0, ())
         multiply_and_evacuate(1, 0)
         banks = begin()
         turn_rows(w_rows(2, 1), banks, 0)

@@ -39,6 +39,8 @@ def tile_hierarchicalattention_pb_kernel(tc, ctx_heads, Wo, bo, features, ln_g, 
 
         vrow = const.tile([P, H], BF16, name="vrow")
         nc.vector.memset(vrow[:], 0.0)
+        vrow_gb = const.tile([P, H], BF16, name="vrow_gb")
+        nc.vector.memset(vrow_gb[:], 0.0)
         gb_rows = const.tile([P, P], BF16, name="gb_rows")
         nc.vector.memset(gb_rows[:], 0.0)
         ident = const.tile([P, P], F32, name="ident")
@@ -78,10 +80,7 @@ def tile_hierarchicalattention_pb_kernel(tc, ctx_heads, Wo, bo, features, ln_g, 
         with tc.manual_schedule(engines={mybir.EngineType.SP}):
             load_w(0, 0)
             load_w(0, 1)
-            for j, vec in enumerate((bo, ln_g, ln_b)):
-                nc.sync.dma_start(out=vrow[32 * j : 32 * j + 1, :], in_=vec.rearrange("(o n) -> o n", o=1))
-            nc.sync.dma_start(out=gb_rows[0:12, :], in_=ln_g.rearrange("(j p) -> j p", p=P))
-            nc.sync.dma_start(out=gb_rows[32:44, :], in_=ln_b.rearrange("(j p) -> j p", p=P))
+            nc.sync.dma_start(out=vrow[0:1, :], in_=bo.rearrange("(o n) -> o n", o=1))
             load_x(0)
             load_x(1)
             load_f(0)
@@ -93,8 +92,11 @@ def tile_hierarchicalattention_pb_kernel(tc, ctx_heads, Wo, bo, features, ln_g, 
             load_w(2, 0)
             load_w(2, 1)
             load_f(2)
+            for j, vec in ((1, ln_g), (2, ln_b)):
+                nc.sync.dma_start(out=vrow_gb[32 * j : 32 * j + 1, :], in_=vec.rearrange("(o n) -> o n", o=1))
+            nc.sync.dma_start(out=gb_rows[0:12, :], in_=ln_g.rearrange("(j p) -> j p", p=P))
+            nc.sync.dma_start(out=gb_rows[32:44, :], in_=ln_b.rearrange("(j p) -> j p", p=P))
 
-        ctx.enter_context(tc.manual_schedule(engines={mybir.EngineType.PE}))
 
         bc = const.tile([P, H], BF16, name="bc")
 
@@ -125,7 +127,7 @@ def tile_hierarchicalattention_pb_kernel(tc, ctx_heads, Wo, bo, features, ln_g, 
                     nc.tensor.matmul(
                         out=pg[:, N_TILE * k : N_TILE * (k + 1)],
                         lhsT=sel[:, j, :],
-                        rhs=vrow[:, SCALAR_COLS + N_TILE * k : SCALAR_COLS + N_TILE * (k + 1)],
+                        rhs=vrow_gb[:, SCALAR_COLS + N_TILE * k : SCALAR_COLS + N_TILE * (k + 1)],
                         start=True,
                         stop=True,
                     )
@@ -260,18 +262,24 @@ def tile_hierarchicalattention_pb_kernel(tc, ctx_heads, Wo, bo, features, ln_g, 
 
         def statistics(b0):
             bs = slice(b0, b0 + 2)
-            mean = small.tile([P, 2], F32, name="mean")
+            negmean = small.tile([P, 2], F32, name="negmean")
             nc.vector.scalar_tensor_tensor(
-                out=mean[:], in0=stats[:, 0, bs, 2], scalar=1.0 / H, in1=part[:, 0, bs], op0=ALU.mult, op1=ALU.add
+                out=negmean[:], in0=stats[:, 0, bs, 2], scalar=-1.0 / H, in1=part[:, 0, bs], op0=ALU.mult, op1=ALU.subtract
             )
             dev = small.tile([P, 2], F32, name="dev")
             nc.vector.scalar_tensor_tensor(
                 out=dev[:], in0=stats[:, 0, bs, 2], scalar=1.0 / H, in1=dev01[:, bs], op0=ALU.mult, op1=ALU.add
             )
-            dev2 = small.tile([P, 2], F32, name="dev2")
-            nc.vector.tensor_tensor(out=dev2[:], in0=dev[:], in1=dev[:], op=ALU.mult)
             nvar = small.tile([P, 2], F32, name="nvar")
-            nc.vector.tensor_tensor(out=nvar[:], in0=dev2[:], in1=var01[:, bs], op=ALU.subtract)
+            for k in range(2):
+                nc.vector.tensor_scalar(
+                    out=nvar[:, k : k + 1],
+                    in0=dev[:, k : k + 1],
+                    scalar1=dev[:, k : k + 1],
+                    scalar2=var01[:, b0 + k : b0 + k + 1],
+                    op0=ALU.mult,
+                    op1=ALU.subtract,
+                )
             rstd = small.tile([P, 2], F32, name="rstd")
             for k in range(2):
                 nc.scalar.activation(
@@ -281,30 +289,30 @@ def tile_hierarchicalattention_pb_kernel(tc, ctx_heads, Wo, bo, features, ln_g, 
                     bias=nvar[:, k : k + 1],
                     scale=-1.0 / H,
                 )
-            shift = small.tile([P, 2], F32, name="shift")
-            nc.vector.scalar_tensor_tensor(
-                out=shift[:], in0=mean[:], scalar=-1.0, in1=rstd[:], op0=ALU.mult, op1=ALU.mult
-            )
             for k in range(2):
-                moments[b0 + k] = (mean[:, k : k + 1], rstd[:, k : k + 1], shift[:, k : k + 1])
+                moments[b0 + k] = (negmean[:, k : k + 1], rstd[:, k : k + 1])
 
         def vector_share(b):
-            mean, rstd, shift = moments[b]
+            negmean, rstd = moments[b]
             v0 = SCALAR_COLS
-            t = work.tile([P, H - SCALAR_COLS], F32, name="t")
+            t = work.tile([P, H - SCALAR_COLS], F32, name="t", bufs=4)
             nc.vector.scalar_tensor_tensor(
-                out=t[:], in0=y[b][:, v0:], scalar=mean, in1=gain_bias[1][:], op0=ALU.subtract, op1=ALU.mult
+                out=t[:], in0=y[b][:, v0:], scalar=negmean, in1=gain_bias[1][:], op0=ALU.add, op1=ALU.mult
             )
-            o = work.tile([P, H - SCALAR_COLS], F32, name="o")
-            nc.vector.scalar_tensor_tensor(
-                out=o[:], in0=t[:], scalar=rstd, in1=gain_bias[2][:], op0=ALU.mult, op1=ALU.add
-            )
-            nc.sync.dma_start(out=out[b, :, v0:], in_=o[:])
+            for k in range(2):
+                ks = slice(N_TILE * k, N_TILE * (k + 1))
+                o = work.tile([P, N_TILE], F32, name="o", bufs=8)
+                nc.vector.scalar_tensor_tensor(
+                    out=o[:], in0=t[:, ks], scalar=rstd, in1=gain_bias[2][:, ks], op0=ALU.mult, op1=ALU.add
+                )
+                nc.sync.dma_start(out=out[b, :, v0 + N_TILE * k : v0 + N_TILE * (k + 1)], in_=o[:])
 
         def normalise(b):
-            mean, rstd, shift = moments[b]
-            z = work.tile([P, SCALAR_COLS], F32, name="z")
-            nc.scalar.activation(out=z[:], in_=y[b][:, :SCALAR_COLS], func=ACT.Identity, bias=shift, scale=rstd)
+            negmean, rstd = moments[b]
+            z = work.tile([P, SCALAR_COLS], F32, name="z", bufs=4)
+            nc.gpsimd.tensor_scalar(
+                out=z[:], in0=y[b][:, :SCALAR_COLS], scalar1=negmean, scalar2=rstd, op0=ALU.add, op1=ALU.mult
+            )
             z_tiles[b] = z
 
         def turn(b):
@@ -314,7 +322,7 @@ def tile_hierarchicalattention_pb_kernel(tc, ctx_heads, Wo, bo, features, ln_g, 
             zt_banks[b] = zt
 
         def gain_and_bias(b):
-            ot = work.tile([P, 4, P], F32, name="ot")
+            ot = work.tile([P, 4, P], F32, name="ot", bufs=4)
             for j in range(4):
                 nc.scalar.activation(
                     out=ot[:, j, :],
@@ -332,7 +340,7 @@ def tile_hierarchicalattention_pb_kernel(tc, ctx_heads, Wo, bo, features, ln_g, 
             back_banks[b] = bk
 
         def scalar_store(b):
-            o_s = work.tile([P, SCALAR_COLS], F32, name="o_s")
+            o_s = work.tile([P, SCALAR_COLS], F32, name="o_s", bufs=4)
             nc.scalar.copy(out=o_s[:], in_=back_banks[b][:].rearrange("p j r -> p (j r)"))
             nc.sync.dma_start(out=out[b, :, :SCALAR_COLS], in_=o_s[:])
 
@@ -340,59 +348,63 @@ def tile_hierarchicalattention_pb_kernel(tc, ctx_heads, Wo, bo, features, ln_g, 
             multiply(c, b)
             evacuate(c, b)
 
-        prepare_w(0, 0, (1, 2))
-        prepare_w(0, 1, (1, 2))
-        columns_of_gain_and_bias()
-        broadcast_bias([0])
-        add_bias(0, nc.vector)
-        prepare_x(0, (1,))
-        broadcast_bias([1, 2])
-        add_bias(1, nc.gpsimd)
-        add_bias(2, nc.gpsimd)
-        prepare_w(1, 0, ())
-        multiply_and_evacuate(0, 0)
-        prepare_x(1, ())
-        multiply_and_evacuate(0, 1)
-        prepare_w(1, 1, ())
-        multiply_and_evacuate(0, 2)
-        banks = begin()
-        turn_rows(w_rows(2, 0), banks, 0)
-        multiply_and_evacuate(0, 3)
-        turn_rows(w_rows(2, 0), banks, 1)
-        finish_w(banks, 2, 0, ())
-        multiply_and_evacuate(1, 0)
-        banks = begin()
-        turn_rows(w_rows(2, 1), banks, 0)
-        multiply_and_evacuate(1, 1)
-        turn_rows(w_rows(2, 1), banks, 1)
-        finish_w(banks, 2, 1, (1,))
-        multiply_and_evacuate(1, 2)
-        multiply_and_evacuate(1, 3)
-        partial_statistics()
-        for b in range(B):
-            multiply(2, b)
-        broadcast_gain_and_bias()
-        evacuate(2, 0)
-        evacuate(2, 1)
-        statistics(0)
-        evacuate(2, 2)
-        evacuate(2, 3)
-        for b in (0, 1):
-            normalise(b)
-            turn(b)
-        statistics(2)
-        for b in (0, 1):
-            gain_and_bias(b)
-            turn_back(b)
-        for b in (2, 3):
-            normalise(b)
-            turn(b)
-        for b in (0, 1):
-            scalar_store(b)
-            vector_share(b)
-        for b in (2, 3):
-            gain_and_bias(b)
-            turn_back(b)
-        for b in (2, 3):
-            vector_share(b)
-            scalar_store(b)
+        with tc.manual_schedule(engines={mybir.EngineType.PE}):
+            prepare_w(0, 0, (1, 2))
+            prepare_w(0, 1, (1, 2))
+            broadcast_bias([0])
+            add_bias(0, nc.vector)
+            prepare_x(0, (1,))
+            broadcast_bias([1, 2])
+            add_bias(1, nc.gpsimd)
+            add_bias(2, nc.gpsimd)
+            prepare_w(1, 0, ())
+            multiply_and_evacuate(0, 0)
+            prepare_x(1, ())
+            multiply_and_evacuate(0, 1)
+            prepare_w(1, 1, ())
+            multiply_and_evacuate(0, 2)
+            banks = begin()
+            turn_rows(w_rows(2, 0), banks, 0)
+            multiply_and_evacuate(0, 3)
+            turn_rows(w_rows(2, 0), banks, 1)
+            finish_w(banks, 2, 0, ())
+            multiply_and_evacuate(1, 0)
+            banks = begin()
+            turn_rows(w_rows(2, 1), banks, 0)
+            multiply_and_evacuate(1, 1)
+            turn_rows(w_rows(2, 1), banks, 1)
+            finish_w(banks, 2, 1, (1,))
+            multiply_and_evacuate(1, 2)
+            multiply_and_evacuate(1, 3)
+            partial_statistics()
+            for b in range(B):
+                multiply(2, b)
+            broadcast_gain_and_bias()
+            columns_of_gain_and_bias()
+        with tc.manual_schedule(engines={mybir.EngineType.PE}):
+            evacuate(2, 0)
+            evacuate(2, 1)
+            statistics(0)
+            vector_share(0)
+            evacuate(2, 2)
+            evacuate(2, 3)
+            statistics(2)
+        with tc.manual_schedule(engines={mybir.EngineType.PE}):
+            for b in (0, 1):
+                normalise(b)
+                turn(b)
+            for b in (0, 1):
+                gain_and_bias(b)
+                turn_back(b)
+            for b in (2, 3):
+                normalise(b)
+                turn(b)
+            scalar_store(0)
+            scalar_store(1)
+            vector_share(1)
+            for b in (2, 3):
+                gain_and_bias(b)
+                turn_back(b)
+            for b in (2, 3):
+                vector_share(b)
+                scalar_store(b)

@@ -23,6 +23,7 @@ N_TILE = 512
 PASSES = A // K_PASS
 CHUNKS = H // N_TILE
 SCALAR_COLS = N_TILE
+WARM_UP = 4
 
 
 def tile_hierarchicalattention_pb_kernel(tc, ctx_heads, Wo, bo, features, ln_g, ln_b, out):
@@ -37,6 +38,8 @@ def tile_hierarchicalattention_pb_kernel(tc, ctx_heads, Wo, bo, features, ln_g, 
         tp_pool = ctx.enter_context(tc.psum_pool(name="tp", bufs=5))
         acc_pool = ctx.enter_context(tc.psum_pool(name="accp", bufs=3))
 
+        zeros = const.tile([P, N_TILE], BF16, name="zeros")
+        nc.vector.memset(zeros[:], 0.0)
         vrow = const.tile([P, H], BF16, name="vrow")
         nc.vector.memset(vrow[:], 0.0)
         vrow_gb = const.tile([P, H], BF16, name="vrow_gb")
@@ -344,11 +347,17 @@ def tile_hierarchicalattention_pb_kernel(tc, ctx_heads, Wo, bo, features, ln_g, 
             nc.scalar.copy(out=o_s[:], in_=back_banks[b][:].rearrange("p j r -> p (j r)"))
             nc.sync.dma_start(out=out[b, :, :SCALAR_COLS], in_=o_s[:])
 
+        def warm_up():
+            idle = tp_pool.tile([P, N_TILE], F32, name="idle", tag="tp")
+            for i in range(WARM_UP):
+                nc.tensor.matmul(out=idle[:], lhsT=zeros[:, :P], rhs=zeros[:], start=True, stop=True)
+
         def multiply_and_evacuate(c, b):
             multiply(c, b)
             evacuate(c, b)
 
         with tc.manual_schedule(engines={mybir.EngineType.PE}):
+            warm_up()
             prepare_w(0, 0, (1, 2))
             prepare_w(0, 1, (1, 2))
             broadcast_bias([0])

@@ -298,17 +298,18 @@ def tile_hierarchicalattention_pb_kernel(tc, ctx_heads, Wo, bo, features, ln_g, 
         def vector_share(b):
             negmean, rstd = moments[b]
             v0 = SCALAR_COLS
-            t = work.tile([P, H - SCALAR_COLS], F32, name="t", bufs=4)
-            nc.vector.scalar_tensor_tensor(
-                out=t[:], in0=y[b][:, v0:], scalar=negmean, in1=gain_bias[1][:], op0=ALU.add, op1=ALU.mult
-            )
             for k in range(2):
                 ks = slice(N_TILE * k, N_TILE * (k + 1))
+                cs = slice(v0 + N_TILE * k, v0 + N_TILE * (k + 1))
+                t = work.tile([P, N_TILE], F32, name="t", bufs=8)
+                nc.vector.scalar_tensor_tensor(
+                    out=t[:], in0=y[b][:, cs], scalar=negmean, in1=gain_bias[1][:, ks], op0=ALU.add, op1=ALU.mult
+                )
                 o = work.tile([P, N_TILE], F32, name="o", bufs=8)
                 nc.vector.scalar_tensor_tensor(
-                    out=o[:], in0=t[:, ks], scalar=rstd, in1=gain_bias[2][:, ks], op0=ALU.mult, op1=ALU.add
+                    out=o[:], in0=t[:], scalar=rstd, in1=gain_bias[2][:, ks], op0=ALU.mult, op1=ALU.add
                 )
-                nc.sync.dma_start(out=out[b, :, v0 + N_TILE * k : v0 + N_TILE * (k + 1)], in_=o[:])
+                nc.sync.dma_start(out=out[b, :, cs], in_=o[:])
 
         def normalise(b):
             negmean, rstd = moments[b]
@@ -345,7 +346,7 @@ def tile_hierarchicalattention_pb_kernel(tc, ctx_heads, Wo, bo, features, ln_g, 
         def scalar_store(b):
             o_s = work.tile([P, SCALAR_COLS], F32, name="o_s", bufs=4)
             nc.scalar.copy(out=o_s[:], in_=back_banks[b][:].rearrange("p j r -> p (j r)"))
-            nc.sync.dma_start(out=out[b, :, :SCALAR_COLS], in_=o_s[:])
+            nc.scalar.dma_start(out=out[b, :, :SCALAR_COLS], in_=o_s[:])
 
         def warm_up():
             idle = tp_pool.tile([P, N_TILE], F32, name="idle", tag="tp")

@@ -369,7 +369,7 @@ def tile_hierarchicalattention_pb_kernel(tc, ctx_heads, Wo, bo, features, ln_g, 
             add_bias(2, nc.gpsimd)
             prepare_w(1, 0, ())
             multiply_and_evacuate(0, 0)
-            prepare_x(1, ())
+            prepare_x(1, (2,))
             multiply_and_evacuate(0, 1)
             prepare_w(1, 1, ())
             multiply_and_evacuate(0, 2)
@@ -377,7 +377,7 @@ def tile_hierarchicalattention_pb_kernel(tc, ctx_heads, Wo, bo, features, ln_g, 
             turn_rows(w_rows(2, 0), banks, 0)
             multiply_and_evacuate(0, 3)
             turn_rows(w_rows(2, 0), banks, 1)
-            finish_w(banks, 2, 0, ())
+            finish_w(banks, 2, 0, (2,))
             multiply_and_evacuate(1, 0)
             banks = begin()
             turn_rows(w_rows(2, 1), banks, 0)
@@ -391,7 +391,7 @@ def tile_hierarchicalattention_pb_kernel(tc, ctx_heads, Wo, bo, features, ln_g, 
                 multiply(2, b)
             broadcast_gain_and_bias()
             columns_of_gain_and_bias()
-        with tc.manual_schedule(engines={mybir.EngineType.PE}):
+        with tc.manual_schedule(engines={mybir.EngineType.PE, mybir.EngineType.Activation}):
             evacuate(2, 0)
             evacuate(2, 1)
             statistics(0)

@@ -391,14 +391,15 @@ def tile_hierarchicalattention_pb_kernel(tc, ctx_heads, Wo, bo, features, ln_g, 
                 multiply(2, b)
             broadcast_gain_and_bias()
             columns_of_gain_and_bias()
-        with tc.manual_schedule(engines={mybir.EngineType.PE, mybir.EngineType.Activation}):
+        with tc.manual_schedule(engines={mybir.EngineType.PE, mybir.EngineType.Activation, mybir.EngineType.DVE}):
             evacuate(2, 0)
             evacuate(2, 1)
             statistics(0)
-            vector_share(0)
             evacuate(2, 2)
             evacuate(2, 3)
             statistics(2)
+        with tc.manual_schedule(engines={mybir.EngineType.PE}):
+            vector_share(0)
         with tc.manual_schedule(engines={mybir.EngineType.PE}):
             for b in (0, 1):
                 normalise(b)

from contextlib import ExitStack

import concourse.mybir as mybir
from concourse.masks import make_identity

B, S, H, A, NH = 4, 128, 1536, 1536, 12
LN_EPS = 1e-5
FLOPS = 2 * B * S * H * A

F32 = mybir.dt.float32
BF16 = mybir.dt.bfloat16
U32 = mybir.dt.uint32
U8 = mybir.dt.uint8
E4M3X4 = mybir.dt.float8_e4m3fn_x4
E5M2X4 = mybir.dt.float8_e5m2_x4
ALU = mybir.AluOpType
ACT = mybir.ActivationFunctionType
AX = mybir.AxisListType

P = 128
K_PASS = 512
N_TILE = 512
PASSES = A // K_PASS
CHUNKS = H // N_TILE
SCALAR_COLS = N_TILE
WARM_UP = 4


def tile_hierarchicalattention_pb_kernel(tc, ctx_heads, Wo, bo, features, ln_g, ln_b, out):
    nc = tc.nc
    with ExitStack() as ctx:
        const = ctx.enter_context(tc.tile_pool(name="const", bufs=1))
        raw = ctx.enter_context(tc.tile_pool(name="raw", bufs=1))
        stage = ctx.enter_context(tc.tile_pool(name="stage", bufs=6))
        keep = ctx.enter_context(tc.tile_pool(name="keep", bufs=1))
        work = ctx.enter_context(tc.tile_pool(name="work", bufs=2))
        small = ctx.enter_context(tc.tile_pool(name="small", bufs=2))
        tp_pool = ctx.enter_context(tc.psum_pool(name="tp", bufs=5))
        acc_pool = ctx.enter_context(tc.psum_pool(name="accp", bufs=3))

        zeros = const.tile([P, N_TILE], BF16, name="zeros")
        nc.vector.memset(zeros[:], 0.0)
        vrow = const.tile([P, H], BF16, name="vrow")
        nc.vector.memset(vrow[:], 0.0)
        vrow_gb = const.tile([P, H], BF16, name="vrow_gb")
        nc.vector.memset(vrow_gb[:], 0.0)
        gb_rows = const.tile([P, P], BF16, name="gb_rows")
        nc.vector.memset(gb_rows[:], 0.0)
        ident = const.tile([P, P], F32, name="ident")
        make_identity(nc, ident[:])
        ident_bf = const.tile([P, P], BF16, name="ident_bf")
        make_identity(nc, ident_bf[:])
        tiny = const.tile([P, 2], F32, name="tiny")
        nc.vector.memset(tiny[:], 1.0)
        nc.scalar.activation(out=tiny[:, 1:2], in_=tiny[:, 0:1], func=ACT.Abs_reciprocal_sqrt)
        sel = const.tile([P, 3, P], BF16, name="sel")
        nc.vector.memset(sel[:], 0.0)
        for j in range(3):
            nc.vector.memset(sel[32 * j : 32 * j + 1, j, :], 1.0)
        gb_col = const.tile([P, P], F32, name="gb_col")

        x_raw = [raw.tile([P, A], BF16, name="x_raw%d" % b) for b in range(B)]
        w_raw = [[raw.tile([P, A], BF16, name="w_raw%d_%d" % (c, a)) for a in range(4)] for c in range(CHUNKS)]
        f_raw = [raw.tile([P, B, N_TILE], BF16, name="f_raw%d" % c) for c in range(CHUNKS)]

        def load_x(b):
            nc.sync.dma_start(
                out=x_raw[b][:].rearrange("p (h d) -> p h d", h=NH),
                in_=ctx_heads[b].rearrange("h s d -> s h d"),
            )

        def load_w(c, half):
            for a in (2 * half, 2 * half + 1):
                r0 = N_TILE * c + P * a
                nc.sync.dma_start(out=w_raw[c][a][:], in_=Wo[r0 : r0 + P, :])

        def load_f(c):
            nc.sync.dma_start(
                out=f_raw[c][:],
                in_=features.rearrange("b s n -> s b n")[:, :, N_TILE * c : N_TILE * (c + 1)],
            )

        with tc.manual_schedule(engines={mybir.EngineType.SP}):
            load_w(0, 0)
            load_w(0, 1)
            nc.sync.dma_start(out=vrow[0:1, :], in_=bo.rearrange("(o n) -> o n", o=1))
            load_x(0)
            load_x(1)
            load_f(0)
            load_w(1, 0)
            load_x(2)
            load_x(3)
            load_w(1, 1)
            load_f(1)
            load_w(2, 0)
            load_w(2, 1)
            load_f(2)
            for j, vec in ((1, ln_g), (2, ln_b)):
                nc.sync.dma_start(out=vrow_gb[32 * j : 32 * j + 1, :], in_=vec.rearrange("(o n) -> o n", o=1))
            nc.sync.dma_start(out=gb_rows[0:12, :], in_=ln_g.rearrange("(j p) -> j p", p=P))
            nc.sync.dma_start(out=gb_rows[32:44, :], in_=ln_b.rearrange("(j p) -> j p", p=P))


        bc = const.tile([P, H], BF16, name="bc")

        def columns_of_gain_and_bias():
            pcol = tp_pool.tile([P, P], BF16, name="pcol", tag="tp")
            nc.tensor.transpose(pcol[:], gb_rows[:], ident_bf[:])
            nc.vector.tensor_copy(out=gb_col[:], in_=pcol[:])

        def broadcast_bias(chunks):
            pb = tp_pool.tile([P, 1024], BF16, name="pb", tag="tp")
            for k, c in enumerate(chunks):
                nc.tensor.matmul(
                    out=pb[:, N_TILE * k : N_TILE * (k + 1)],
                    lhsT=sel[:, 0, :],
                    rhs=vrow[:, N_TILE * c : N_TILE * (c + 1)],
                    start=True,
                    stop=True,
                )
            ncol = N_TILE * len(chunks)
            nc.scalar.copy(out=bc[:, N_TILE * chunks[0] : N_TILE * chunks[0] + ncol], in_=pb[:, :ncol])

        gain_bias = {}

        def broadcast_gain_and_bias():
            for j in (1, 2):
                pg = tp_pool.tile([P, H - SCALAR_COLS], BF16, name="pg%d" % j, tag="tp")
                for k in range(2):
                    nc.tensor.matmul(
                        out=pg[:, N_TILE * k : N_TILE * (k + 1)],
                        lhsT=sel[:, j, :],
                        rhs=vrow_gb[:, SCALAR_COLS + N_TILE * k : SCALAR_COLS + N_TILE * (k + 1)],
                        start=True,
                        stop=True,
                    )
                gain_bias[j] = pg

        fb = [keep.tile([P, H], F32, name="fb%d" % b) for b in range(B)]

        def add_bias(c, engine):
            cs = slice(N_TILE * c, N_TILE * (c + 1))
            for b in range(B):
                engine.tensor_tensor(out=fb[b][:, cs], in0=f_raw[c][:, b, :], in1=bc[:, cs], op=ALU.add)

        x_codes = [keep.tile([P, N_TILE], U32, name="x_codes%d" % g, align_bytes=64) for g in range(PASSES)]
        x_scales = [keep.tile([P, N_TILE], U8, name="x_scales%d" % g, align_bytes=64) for g in range(PASSES)]
        w_codes = [
            [keep.tile([P, N_TILE], U32, name="w_codes%d_%d" % (c, g), align_bytes=64) for g in range(PASSES)]
            for c in range(CHUNKS)
        ]
        w_scales = [
            [keep.tile([P, N_TILE], U8, name="w_scales%d_%d" % (c, g), align_bytes=64) for g in range(PASSES)]
            for c in range(CHUNKS)
        ]
        y = [keep.tile([P, H], F32, name="y%d" % b) for b in range(B)]
        stats = keep.tile([P, 2, B, CHUNKS], F32, name="stats")
        negc = keep.tile([P, B], F32, name="negc")

        def begin():
            return [tp_pool.tile([P, 2, 2, P], F32, name="tp%d" % g, tag="tp") for g in range(PASSES)]

        def turn_rows(srcs, banks, a):
            for g in range(PASSES):
                words = srcs[a][:, K_PASS * g : K_PASS * (g + 1)].bitcast(F32)
                for u in range(2):
                    nc.tensor.transpose(banks[g][:, a, u, :], words[:, u : K_PASS // 2 : 2], ident[:])

        def finish(banks, codes, scales, fmt, half, vector_passes):
            groups = []
            for g in range(PASSES):
                grouped = stage.tile([P, 2 * N_TILE], BF16, name="grouped", align_bytes=64)
                dst = grouped[:].bitcast(F32).rearrange("p (a r u) -> p a r u", a=2, u=2)
                src = banks[g][:].rearrange("p a u r -> p a r u")
                if g in vector_passes:
                    nc.vector.tensor_copy(out=dst, in_=src)
                else:
                    nc.scalar.copy(out=dst, in_=src)
                groups.append(grouped)
            hs = slice(256 * half, 256 * (half + 1))
            for g in range(PASSES):
                nc.vector.quantize_mx(out=codes[g][:, hs].bitcast(fmt), scales=scales[g][:, hs], in_=groups[g][:])

        def x_rows(half):
            return x_raw[2 * half : 2 * half + 2]

        def w_rows(c, half):
            return w_raw[c][2 * half : 2 * half + 2]

        def finish_x(banks, half, vector_passes):
            finish(banks, x_codes, x_scales, E5M2X4, half, vector_passes)

        def finish_w(banks, c, half, vector_passes):
            finish(banks, w_codes[c], w_scales[c], E4M3X4, half, vector_passes)

        def prepare_x(half, vector_passes):
            banks = begin()
            turn_rows(x_rows(half), banks, 0)
            turn_rows(x_rows(half), banks, 1)
            finish_x(banks, half, vector_passes)

        def prepare_w(c, half, vector_passes):
            banks = begin()
            turn_rows(w_rows(c, half), banks, 0)
            turn_rows(w_rows(c, half), banks, 1)
            finish_w(banks, c, half, vector_passes)

        acc = {}

        def multiply(c, b):
            acc[b] = acc_pool.tile([P, N_TILE], F32, name="acc", tag="acc")
            ts = slice(P * b, P * (b + 1))
            for g in range(PASSES):
                nc.tensor.matmul_mx(
                    out=acc[b][:],
                    lhsT=x_codes[g][:, ts].bitcast(E5M2X4),
                    lhsT_scale=x_scales[g][:, ts],
                    rhs=w_codes[c][g][:].bitcast(E4M3X4),
                    rhs_scale=w_scales[c][g][:],
                    start=(g == 0),
                    stop=(g == PASSES - 1),
                )

        def evacuate(c, b):
            cs = slice(N_TILE * c, N_TILE * (c + 1))
            nc.vector.scalar_tensor_tensor(
                out=y[b][:, cs],
                in0=acc[b][:],
                scalar=1.0,
                in1=fb[b][:, cs],
                op0=ALU.mult,
                op1=ALU.add,
                accum_out=stats[:, 0, b, c : c + 1],
            )
            if c == 0:
                nc.vector.tensor_scalar(
                    out=negc[:, b : b + 1], in0=stats[:, 0, b, 0:1], scalar1=-1.0 / N_TILE, scalar2=None, op0=ALU.mult
                )
            junk = work.tile([P, N_TILE], BF16, name="junk")
            nc.scalar.activation(
                out=junk[:],
                in_=y[b][:, cs],
                func=ACT.Square,
                bias=negc[:, b : b + 1],
                scale=1.0,
                accum_out=stats[:, 1, b, c : c + 1],
            )

        moments = {}
        z_tiles = {}
        zt_banks = {}
        ot_tiles = {}
        back_banks = {}

        part = keep.tile([P, 2, B], F32, name="part")
        dev01 = keep.tile([P, B], F32, name="dev01")
        var01 = keep.tile([P, B], F32, name="var01")

        def partial_statistics():
            red = small.tile([P, 2, B], F32, name="red")
            nc.vector.tensor_reduce(out=red[:], in_=stats[:, :, :, 0:2], axis=AX.X, op=ALU.add)
            nc.vector.tensor_scalar(out=part[:], in0=red[:], scalar1=1.0 / H, scalar2=None, op0=ALU.mult)
            nc.vector.tensor_tensor(out=dev01[:], in0=part[:, 0, :], in1=negc[:], op=ALU.add)
            nc.vector.tensor_scalar(out=var01[:], in0=part[:, 1, :], scalar1=LN_EPS, scalar2=None, op0=ALU.add)

        def statistics(b0):
            bs = slice(b0, b0 + 2)
            negmean = small.tile([P, 2], F32, name="negmean")
            nc.vector.scalar_tensor_tensor(
                out=negmean[:], in0=stats[:, 0, bs, 2], scalar=-1.0 / H, in1=part[:, 0, bs], op0=ALU.mult, op1=ALU.subtract
            )
            dev = small.tile([P, 2], F32, name="dev")
            nc.vector.scalar_tensor_tensor(
                out=dev[:], in0=stats[:, 0, bs, 2], scalar=1.0 / H, in1=dev01[:, bs], op0=ALU.mult, op1=ALU.add
            )
            nvar = small.tile([P, 2], F32, name="nvar")
            for k in range(2):
                nc.vector.tensor_scalar(
                    out=nvar[:, k : k + 1],
                    in0=dev[:, k : k + 1],
                    scalar1=dev[:, k : k + 1],
                    scalar2=var01[:, b0 + k : b0 + k + 1],
                    op0=ALU.mult,
                    op1=ALU.subtract,
                )
            rstd = small.tile([P, 2], F32, name="rstd")
            for k in range(2):
                nc.scalar.activation(
                    out=rstd[:, k : k + 1],
                    in_=stats[:, 1, b0 + k, 2:3],
                    func=ACT.Abs_reciprocal_sqrt,
                    bias=nvar[:, k : k + 1],
                    scale=-1.0 / H,
                )
            for k in range(2):
                moments[b0 + k] = (negmean[:, k : k + 1], rstd[:, k : k + 1])

        def vector_share(b):
            negmean, rstd = moments[b]
            v0 = SCALAR_COLS
            for k in range(2):
                ks = slice(N_TILE * k, N_TILE * (k + 1))
                cs = slice(v0 + N_TILE * k, v0 + N_TILE * (k + 1))
                t = work.tile([P, N_TILE], F32, name="t", bufs=8)
                nc.vector.scalar_tensor_tensor(
                    out=t[:], in0=y[b][:, cs], scalar=negmean, in1=gain_bias[1][:, ks], op0=ALU.add, op1=ALU.mult
                )
                o = work.tile([P, N_TILE], F32, name="o", bufs=8)
                nc.vector.scalar_tensor_tensor(
                    out=o[:], in0=t[:], scalar=rstd, in1=gain_bias[2][:, ks], op0=ALU.mult, op1=ALU.add
                )
                nc.sync.dma_start(out=out[b, :, cs], in_=o[:])

        def normalise(b):
            negmean, rstd = moments[b]
            z = work.tile([P, SCALAR_COLS], F32, name="z", bufs=4)
            nc.gpsimd.tensor_scalar(
                out=z[:], in0=y[b][:, :SCALAR_COLS], scalar1=negmean, scalar2=rstd, op0=ALU.add, op1=ALU.mult
            )
            z_tiles[b] = z

        def turn(b):
            zt = tp_pool.tile([P, 4, P], F32, name="zt", tag="tp")
            for j in range(4):
                nc.tensor.transpose(zt[:, j, :], z_tiles[b][:, P * j : P * (j + 1)], ident[:])
            zt_banks[b] = zt

        def gain_and_bias(b):
            ot = work.tile([P, 4, P], F32, name="ot", bufs=4)
            for j in range(4):
                nc.scalar.activation(
                    out=ot[:, j, :],
                    in_=zt_banks[b][:, j, :],
                    func=ACT.Identity,
                    bias=gb_col[:, 32 + j : 33 + j],
                    scale=gb_col[:, j : j + 1],
                )
            ot_tiles[b] = ot

        def turn_back(b):
            bk = tp_pool.tile([P, 4, P], F32, name="bk", tag="tp")
            for j in range(4):
                nc.tensor.transpose(bk[:, j, :], ot_tiles[b][:, j, :], ident[:])
            back_banks[b] = bk

        def scalar_store(b):
            o_s = work.tile([P, SCALAR_COLS], F32, name="o_s", bufs=4)
            nc.scalar.copy(out=o_s[:], in_=back_banks[b][:].rearrange("p j r -> p (j r)"))
            nc.scalar.dma_start(out=out[b, :, :SCALAR_COLS], in_=o_s[:])

        def warm_up():
            idle = tp_pool.tile([P, N_TILE], F32, name="idle", tag="tp")
            for i in range(WARM_UP):
                nc.tensor.matmul(out=idle[:], lhsT=zeros[:, :P], rhs=zeros[:], start=True, stop=True)

        def multiply_and_evacuate(c, b):
            multiply(c, b)
            evacuate(c, b)

        with tc.manual_schedule(engines={mybir.EngineType.PE}):
            warm_up()
            prepare_w(0, 0, (1, 2))
            prepare_w(0, 1, (1, 2))
            broadcast_bias([0])
            add_bias(0, nc.vector)
            prepare_x(0, (1,))
            broadcast_bias([1, 2])
            add_bias(1, nc.gpsimd)
            add_bias(2, nc.gpsimd)
            prepare_w(1, 0, ())
            multiply_and_evacuate(0, 0)
            prepare_x(1, (2,))
            multiply_and_evacuate(0, 1)
            prepare_w(1, 1, ())
            multiply_and_evacuate(0, 2)
            banks = begin()
            turn_rows(w_rows(2, 0), banks, 0)
            multiply_and_evacuate(0, 3)
            turn_rows(w_rows(2, 0), banks, 1)
            finish_w(banks, 2, 0, (2,))
            multiply_and_evacuate(1, 0)
            banks = begin()
            turn_rows(w_rows(2, 1), banks, 0)
            multiply_and_evacuate(1, 1)
            turn_rows(w_rows(2, 1), banks, 1)
            finish_w(banks, 2, 1, (1,))
            multiply_and_evacuate(1, 2)
            multiply_and_evacuate(1, 3)
            partial_statistics()
            for b in range(B):
                multiply(2, b)
            broadcast_gain_and_bias()
            columns_of_gain_and_bias()
        with tc.manual_schedule(engines={mybir.EngineType.PE, mybir.EngineType.Activation, mybir.EngineType.DVE}):
            evacuate(2, 0)
            evacuate(2, 1)
            statistics(0)
            evacuate(2, 2)
            evacuate(2, 3)
            statistics(2)
        with tc.manual_schedule(engines={mybir.EngineType.PE}):
            vector_share(0)
        with tc.manual_schedule(engines={mybir.EngineType.PE}):
            for b in (0, 1):
                normalise(b)
                turn(b)
            for b in (0, 1):
                gain_and_bias(b)
                turn_back(b)
            for b in (2, 3):
                normalise(b)
                turn(b)
            scalar_store(0)
            scalar_store(1)
            vector_share(1)
            for b in (2, 3):
                gain_and_bias(b)
                turn_back(b)
            for b in (2, 3):
                vector_share(b)
                scalar_store(b)
